import numpy as np
import ml_dtypes


def mxq(x, axis, fmt="e4m3"):
    dtype, down = {"e4m3": (ml_dtypes.float8_e4m3fn, 7), "e5m2": (ml_dtypes.float8_e5m2, 14)}[fmt]
    v = np.moveaxis(np.asarray(x, np.float32).astype(ml_dtypes.bfloat16).astype(np.float64), axis, -1)
    blocks = v.reshape(v.shape[:-1] + (-1, 32))
    amax = np.abs(blocks).max(-1, keepdims=True)
    byte = np.maximum(np.where(amax > 0, np.frexp(amax)[1] - 1 + 127, 0) - down, 1)
    scale = np.exp2(byte - 127.0)
    codes = (blocks / scale).astype(np.float32).astype(dtype).astype(np.float64)
    return np.moveaxis((codes * scale).reshape(v.shape), -1, axis)


WIDE = False


def mx_kscale(k):
    if not WIDE:
        return np.ones(k)
    levels = np.array([10, -10, 5, -5, 0])
    a = np.random.permutation(np.resize(levels, k // 512 * 4)).reshape(k // 512, 4)
    idx = np.arange(k)
    return np.exp2(a[idx // 512, idx % 128 // 32])


BF16 = ml_dtypes.bfloat16


def bf(x):
    return np.asarray(x, np.float32).astype(BF16)


def f64(x):
    return np.asarray(x).astype(np.float64)


B, T, N, D, H = 2, 2, 1024, 512, 4


def setup_inputs():
    t = mx_kscale(D)
    return {"adj": bf(np.random.uniform(size=(N, N)) * 16.0 / N),
            "query": bf(np.random.standard_normal((B, T, N, D)) * 0.8 * t),
            "Wt": bf(np.random.standard_normal((D, D)) * 10.0 / np.sqrt(D) / t),
            "bt": bf(np.random.standard_normal(D) * 0.2)}


def reference(adj, query, Wt, bt):
    A = f64(adj) + np.eye(N)
    nadj = A / A.sum(1, keepdims=True)
    gq = mxq(nadj, 1, "e4m3") @ mxq(f64(query), 2, "e4m3")
    return np.maximum((mxq(gq, 3, "e4m3") @ mxq(f64(Wt), 1, "e4m3").T) + f64(bt), 0.0)

@@ -1,0 +1,226 @@
+from contextlib import ExitStack
+
+import concourse.mybir as mybir
+from concourse.masks import make_identity
+
+F32 = mybir.dt.float32
+BF16 = mybir.dt.bfloat16
+U32 = mybir.dt.uint32
+U8 = mybir.dt.uint8
+FP8X4 = mybir.dt.float8_e4m3fn_x4
+ACT = mybir.ActivationFunctionType
+ALU = mybir.AluOpType
+
+P = 128
+PACK = 4
+K_PASS = P * PACK
+
+NODES = 1024
+FEATURES = 512
+SLICES = 4
+NODE_TILES = NODES // P
+NODE_PASSES = NODES // K_PASS
+FEATURE_TILES = FEATURES // P
+GROUP = 4
+GROUPS = NODE_TILES // GROUP
+
+FLOPS = 2 * SLICES * NODES * NODES * FEATURES + 2 * SLICES * NODES * FEATURES * FEATURES
+
+
+def tile_gatedspatialattentionlayer_pc_t_kernel(tc, adj, query, Wt, bt, out):
+    nc = tc.nc
+    query_slices = query.rearrange("b t n d -> (b t) n d")
+    out_slices = out.rearrange("b t n o -> (b t) n o")
+
+    with ExitStack() as ctx:
+        keep = ctx.enter_context(tc.tile_pool(name="keep", bufs=1))
+        stage = ctx.enter_context(tc.tile_pool(name="stage", bufs=3))
+        results = ctx.enter_context(tc.tile_pool(name="results", bufs=4))
+        psum = ctx.enter_context(tc.psum_pool(name="psum", bufs=4))
+
+        ident_bf = keep.tile([P, P], BF16)
+        make_identity(nc, ident_bf[:])
+        ident_f32 = keep.tile([P, P], F32)
+        make_identity(nc, ident_f32[:])
+
+        adj_sb = keep.tile([P, NODE_TILES, NODES], BF16)
+        query_sb = keep.tile([P, SLICES, NODES // P, FEATURES], BF16)
+        wt_sb = keep.tile([P, FEATURE_TILES, FEATURES], BF16)
+        bias_sb = keep.tile([P, FEATURES], BF16)
+        row_sum = keep.tile([P, NODE_TILES], F32)
+        denominator = keep.tile([P, NODE_TILES], F32)
+        inv_sum = keep.tile([P, NODE_TILES], F32)
+
+        nadj_codes = keep.tile([P, NODE_TILES, NODE_PASSES, P], U32, align_bytes=64)
+        nadj_scales = keep.tile([P, NODE_TILES, NODE_PASSES, P], U8, align_bytes=64)
+        query_codes = keep.tile([P, SLICES, NODE_PASSES, FEATURES], U32, align_bytes=64)
+        query_scales = keep.tile([P, SLICES, NODE_PASSES, FEATURES], U8, align_bytes=64)
+        wt_codes = keep.tile([P, FEATURES], U32, align_bytes=64)
+        wt_scales = keep.tile([P, FEATURES], U8, align_bytes=64)
+
+        def load_adj(i):
+            nc.sync.dma_start(out=adj_sb[:, i, :], in_=adj[i * P : (i + 1) * P, :])
+
+        def load_query(s, g):
+            rows = query_slices[s].rearrange("(j p) d -> p j d", p=P)
+            j_range = slice(g * PACK, (g + 1) * PACK)
+            nc.sync.dma_start(out=query_sb[:, s, j_range, :], in_=rows[:, j_range, :])
+
+        load_adj(0)
+        load_query(0, 0)
+        load_adj(1)
+        load_query(0, 1)
+        for i in range(2, NODE_TILES):
+            load_adj(i)
+        nc.sync.dma_start(out=wt_sb[:], in_=Wt.rearrange("(a p) d -> p a d", p=P))
+        nc.sync.dma_start(out=bias_sb[:], in_=bt.partition_broadcast(P))
+        for s in range(1, SLICES):
+            for g in range(NODE_PASSES):
+                load_query(s, g)
+
+        def quantise_query(s):
+            for g in range(NODE_PASSES):
+                grouped = stage.tile([P, FEATURES, PACK], BF16, align_bytes=64, name="query_grouped")
+                copy = nc.vector.tensor_copy if g % 2 == 0 else nc.scalar.copy
+                copy(
+                    out=grouped[:].rearrange("p (c i) t -> p c t i", i=4),
+                    in_=query_sb[:, s, g * PACK : (g + 1) * PACK, :].rearrange(
+                        "p t (c i) -> p c t i", i=4
+                    ),
+                )
+                nc.vector.quantize_mx(
+                    out=query_codes[:, s, g, :].bitcast(FP8X4),
+                    scales=query_scales[:, s, g, :],
+                    in_=grouped[:].rearrange("p d t -> p (d t)"),
+                )
+
+        def transpose_512(block, diagonal_t):
+            flipped = psum.tile([P, PACK, P], F32, name="flipped", tag="quad")
+            for t in range(PACK):
+                nc.tensor.matmul(
+                    out=flipped[:, t, :],
+                    lhsT=block[:, t * P : (t + 1) * P],
+                    rhs=ident_bf[:],
+                    start=True,
+                    stop=(t != diagonal_t),
+                )
+                if t == diagonal_t:
+                    nc.tensor.matmul(
+                        out=flipped[:, t, :], lhsT=ident_bf[:], rhs=ident_bf[:], start=False, stop=True
+                    )
+            return flipped
+
+        def quantise_nadj(i):
+            unread = stage.tile([P, NODES], BF16, name="unread")
+            nc.scalar.activation(
+                out=unread[:], in_=adj_sb[:, i, :], func=ACT.Copy, accum_out=row_sum[:, i : i + 1]
+            )
+            nc.vector.tensor_scalar_add(
+                out=denominator[:, i : i + 1], in0=row_sum[:, i : i + 1], scalar1=1.0
+            )
+            nc.vector.reciprocal(out=inv_sum[:, i : i + 1], in_=denominator[:, i : i + 1])
+            spread_ps = psum.tile([P, P], F32, name="spread_ps", tag="wide")
+            nc.tensor.matmul(
+                out=spread_ps[:],
+                lhsT=inv_sum[:, i : i + 1].to_broadcast([P, P]),
+                rhs=ident_f32[:],
+                start=True,
+                stop=True,
+            )
+            spread = stage.tile([P, P], F32, name="spread")
+            nc.scalar.copy(out=spread[:], in_=spread_ps[:])
+
+            grouped = stage.tile([P, NODE_PASSES, P, PACK], BF16, align_bytes=64, name="nadj_grouped")
+            for g in range(NODE_PASSES):
+                diagonal_t = i - g * PACK if g == i // PACK else None
+                flipped = transpose_512(adj_sb[:, i, g * K_PASS : (g + 1) * K_PASS], diagonal_t)
+                nc.vector.tensor_tensor(
+                    out=grouped[:, g, :, :],
+                    in0=flipped[:].rearrange("p t r -> p r t"),
+                    in1=spread[:].unsqueeze(2).to_broadcast([P, P, PACK]),
+                    op=ALU.mult,
+                )
+            nc.vector.quantize_mx(
+                out=nadj_codes[:, i, :, :].rearrange("p g r -> p (g r)").bitcast(FP8X4),
+                scales=nadj_scales[:, i, :, :].rearrange("p g r -> p (g r)"),
+                in_=grouped[:].rearrange("p g r t -> p (g r t)"),
+            )
+
+        def quantise_wt():
+            grouped = keep.tile([P, FEATURE_TILES, P, PACK], BF16, align_bytes=64, name="wt_grouped")
+            for a in range(FEATURE_TILES):
+                flipped = transpose_512(wt_sb[:, a, :], None)
+                nc.scalar.copy(out=grouped[:, a, :, :], in_=flipped[:].rearrange("p t r -> p r t"))
+            nc.vector.quantize_mx(
+                out=wt_codes[:].bitcast(FP8X4),
+                scales=wt_scales[:],
+                in_=grouped[:].rearrange("p a r t -> p (a r t)"),
+            )
+
+        def aggregate(s, h):
+            grouped = stage.tile([P, GROUP, P, PACK], BF16, align_bytes=64, name="gq_grouped")
+            for c in range(GROUP):
+                i = h * GROUP + c
+                gq_ps = psum.tile([P, FEATURE_TILES, P], F32, name="gq_ps", tag="quad")
+                for t in range(FEATURE_TILES):
+                    for g in range(NODE_PASSES):
+                        nc.tensor.matmul_mx(
+                            out=gq_ps[:, t, :],
+                            lhsT=query_codes[:, s, g, t * P : (t + 1) * P].bitcast(FP8X4),
+                            lhsT_scale=query_scales[:, s, g, t * P : (t + 1) * P],
+                            rhs=nadj_codes[:, i, g, :].bitcast(FP8X4),
+                            rhs_scale=nadj_scales[:, i, g, :],
+                            start=(g == 0),
+                            stop=(g == NODE_PASSES - 1),
+                        )
+                nc.scalar.copy(out=grouped[:, c, :, :], in_=gq_ps[:].rearrange("p t r -> p r t"))
+            gq_codes = stage.tile([P, GROUP * P], U32, align_bytes=64, name="gq_codes")
+            gq_scales = stage.tile([P, GROUP * P], U8, align_bytes=64, name="gq_scales")
+            nc.vector.quantize_mx(
+                out=gq_codes[:].bitcast(FP8X4),
+                scales=gq_scales[:],
+                in_=grouped[:].rearrange("p c r t -> p (c r t)"),
+            )
+            return gq_codes, gq_scales
+
+        def project(s, h, gq_codes, gq_scales):
+            for c in range(GROUP):
+                i = h * GROUP + c
+                out_ps = psum.tile([P, FEATURES], F32, name="out_ps", tag="wide")
+                nc.tensor.matmul_mx(
+                    out=out_ps[:],
+                    lhsT=gq_codes[:, c * P : (c + 1) * P].bitcast(FP8X4),
+                    lhsT_scale=gq_scales[:, c * P : (c + 1) * P],
+                    rhs=wt_codes[:].bitcast(FP8X4),
+                    rhs_scale=wt_scales[:],
+                    start=True,
+                    stop=True,
+                )
+                biased = results.tile([P, FEATURES], F32, name="biased")
+                nc.vector.tensor_tensor(out=biased[:], in0=out_ps[:], in1=bias_sb[:], op=ALU.add)
+                result = results.tile([P, FEATURES], F32, name="result")
+                nc.gpsimd.tensor_scalar(
+                    out=result[:],
+                    in0=biased[:],
+                    scalar1=float("inf"),
+                    scalar2=0.0,
+                    op0=ALU.min,
+                    op1=ALU.max,
+                )
+                nc.sync.dma_start(out=out_slices[s, i * P : (i + 1) * P, :], in_=result[:])
+
+        quantise_query(0)
+        for i in range(NODE_TILES):
+            quantise_nadj(i)
+        quantise_wt()
+
+        pending = None
+        for s in range(SLICES):
+            for h in range(GROUPS):
+                codes_and_scales = aggregate(s, h)
+                if h == 0 and s + 1 < SLICES:
+                    quantise_query(s + 1)
+                if pending is not None:
+                    project(*pending)
+                pending = (s, h) + codes_and_scales
+        project(*pending)

@@ -81,8 +81,7 @@ def tile_gatedspatialattentionlayer_pc_t_kernel(tc, adj, query, Wt, bt, out):
         def quantise_query(s):
             for g in range(NODE_PASSES):
                 grouped = stage.tile([P, FEATURES, PACK], BF16, align_bytes=64, name="query_grouped")
-                copy = nc.vector.tensor_copy if g % 2 == 0 else nc.scalar.copy
-                copy(
+                nc.vector.tensor_copy(
                     out=grouped[:].rearrange("p (c i) t -> p c t i", i=4),
                     in_=query_sb[:, s, g * PACK : (g + 1) * PACK, :].rearrange(
                         "p t (c i) -> p c t i", i=4
@@ -199,14 +198,7 @@ def tile_gatedspatialattentionlayer_pc_t_kernel(tc, adj, query, Wt, bt, out):
                 biased = results.tile([P, FEATURES], F32, name="biased")
                 nc.vector.tensor_tensor(out=biased[:], in0=out_ps[:], in1=bias_sb[:], op=ALU.add)
                 result = results.tile([P, FEATURES], F32, name="result")
-                nc.gpsimd.tensor_scalar(
-                    out=result[:],
-                    in0=biased[:],
-                    scalar1=float("inf"),
-                    scalar2=0.0,
-                    op0=ALU.min,
-                    op1=ALU.max,
-                )
+                nc.scalar.activation(out=result[:], in_=biased[:], func=ACT.Relu)
                 nc.sync.dma_start(out=out_slices[s, i * P : (i + 1) * P, :], in_=result[:])
 
         quantise_query(0)

@@ -23,6 +23,7 @@ NODE_PASSES = NODES // K_PASS
 FEATURE_TILES = FEATURES // P
 GROUP = 4
 GROUPS = NODE_TILES // GROUP
+GPSIMD_TILES = 2
 
 FLOPS = 2 * SLICES * NODES * NODES * FEATURES + 2 * SLICES * NODES * FEATURES * FEATURES
 
@@ -36,6 +37,7 @@ def tile_gatedspatialattentionlayer_pc_t_kernel(tc, adj, query, Wt, bt, out):
         keep = ctx.enter_context(tc.tile_pool(name="keep", bufs=1))
         stage = ctx.enter_context(tc.tile_pool(name="stage", bufs=3))
         results = ctx.enter_context(tc.tile_pool(name="results", bufs=4))
+        own = ctx.enter_context(tc.tile_pool(name="own", bufs=SLICES * GROUPS * GPSIMD_TILES))
         psum = ctx.enter_context(tc.psum_pool(name="psum", bufs=4))
 
         ident_bf = keep.tile([P, P], BF16)
@@ -81,7 +83,8 @@ def tile_gatedspatialattentionlayer_pc_t_kernel(tc, adj, query, Wt, bt, out):
         def quantise_query(s):
             for g in range(NODE_PASSES):
                 grouped = stage.tile([P, FEATURES, PACK], BF16, align_bytes=64, name="query_grouped")
-                nc.vector.tensor_copy(
+                copy = nc.vector.tensor_copy if s == 0 or g % 2 == 0 else nc.scalar.copy
+                copy(
                     out=grouped[:].rearrange("p (c i) t -> p c t i", i=4),
                     in_=query_sb[:, s, g * PACK : (g + 1) * PACK, :].rearrange(
                         "p t (c i) -> p c t i", i=4
@@ -195,11 +198,25 @@ def tile_gatedspatialattentionlayer_pc_t_kernel(tc, adj, query, Wt, bt, out):
                     start=True,
                     stop=True,
                 )
-                biased = results.tile([P, FEATURES], F32, name="biased")
-                nc.vector.tensor_tensor(out=biased[:], in0=out_ps[:], in1=bias_sb[:], op=ALU.add)
-                result = results.tile([P, FEATURES], F32, name="result")
-                nc.scalar.activation(out=result[:], in_=biased[:], func=ACT.Relu)
-                nc.sync.dma_start(out=out_slices[s, i * P : (i + 1) * P, :], in_=result[:])
+                rows = out_slices[s, i * P : (i + 1) * P, :]
+                if c < GPSIMD_TILES:
+                    result = own.tile([P, FEATURES], F32, name="own_result")
+                    nc.vector.tensor_tensor(out=result[:], in0=out_ps[:], in1=bias_sb[:], op=ALU.add)
+                    nc.gpsimd.tensor_scalar(
+                        out=result[:],
+                        in0=result[:],
+                        scalar1=float("inf"),
+                        scalar2=0.0,
+                        op0=ALU.min,
+                        op1=ALU.max,
+                    )
+                    nc.gpsimd.dma_start(out=rows, in_=result[:])
+                else:
+                    biased = results.tile([P, FEATURES], F32, name="biased")
+                    nc.vector.tensor_tensor(out=biased[:], in0=out_ps[:], in1=bias_sb[:], op=ALU.add)
+                    result = results.tile([P, FEATURES], F32, name="result")
+                    nc.scalar.activation(out=result[:], in_=biased[:], func=ACT.Relu)
+                    nc.sync.dma_start(out=rows, in_=result[:])
 
         quantise_query(0)
         for i in range(NODE_TILES):

@@ -21,9 +21,49 @@ SLICES = 4
 NODE_TILES = NODES // P
 NODE_PASSES = NODES // K_PASS
 FEATURE_TILES = FEATURES // P
-GROUP = 4
-GROUPS = NODE_TILES // GROUP
-GPSIMD_TILES = 2
+GROUP_SIZES = (4, 4, 4, 4, 4, 4, 4, 2, 2)
+LAG = {
+    "fold": 0,
+    "sum": 1,
+    "invert": 2,
+    "norm": 2,
+    "diag": 3,
+    "flip": 4,
+    "words": 5,
+    "qnadj": 6,
+    "aggregate": 7,
+    "evacuate": 8,
+}
+EXTRA_WORK = (
+    (0, 0, "regroup0"),
+    (2, 0, "quantise0"),
+    (3, 0, "regroup1v"),
+    (5, 0, "quantise1"),
+    (7, 0, "flip_wt"),
+    (8, 1, "flip_wt"),
+    (9, 2, "flip_wt"),
+    (10, 3, "flip_wt"),
+    (8, 0, "copy_wt"),
+    (9, 1, "copy_wt"),
+    (10, 2, "copy_wt"),
+    (11, 3, "copy_wt"),
+    (12, 0, "quantise_wt"),
+    (9, 1, "regroup0"),
+    (10, 1, "regroup1a"),
+    (11, 1, "quantise0"),
+    (12, 1, "regroup1b"),
+    (14, 1, "quantise1"),
+    (17, 2, "regroup0"),
+    (18, 2, "regroup1a"),
+    (19, 2, "quantise0"),
+    (20, 2, "regroup1b"),
+    (22, 2, "quantise1"),
+    (25, 3, "regroup0"),
+    (26, 3, "regroup1a"),
+    (27, 3, "quantise0"),
+    (28, 3, "regroup1b"),
+    (30, 3, "quantise1"),
+)
 
 FLOPS = 2 * SLICES * NODES * NODES * FEATURES + 2 * SLICES * NODES * FEATURES * FEATURES
 
@@ -35,9 +75,8 @@ def tile_gatedspatialattentionlayer_pc_t_kernel(tc, adj, query, Wt, bt, out):
 
     with ExitStack() as ctx:
         keep = ctx.enter_context(tc.tile_pool(name="keep", bufs=1))
-        stage = ctx.enter_context(tc.tile_pool(name="stage", bufs=3))
-        results = ctx.enter_context(tc.tile_pool(name="results", bufs=4))
-        own = ctx.enter_context(tc.tile_pool(name="own", bufs=SLICES * GROUPS * GPSIMD_TILES))
+        stage = ctx.enter_context(tc.tile_pool(name="stage", bufs=4))
+        results = ctx.enter_context(tc.tile_pool(name="results", bufs=8))
         psum = ctx.enter_context(tc.psum_pool(name="psum", bufs=4))
 
         ident_bf = keep.tile([P, P], BF16)
@@ -46,17 +85,17 @@ def tile_gatedspatialattentionlayer_pc_t_kernel(tc, adj, query, Wt, bt, out):
         make_identity(nc, ident_f32[:])
 
         adj_sb = keep.tile([P, NODE_TILES, NODES], BF16)
-        query_sb = keep.tile([P, SLICES, NODES // P, FEATURES], BF16)
+        query_sb = keep.tile([P, SLICES, NODE_PASSES, PACK, FEATURES], BF16)
         wt_sb = keep.tile([P, FEATURE_TILES, FEATURES], BF16)
         bias_sb = keep.tile([P, FEATURES], BF16)
         row_sum = keep.tile([P, NODE_TILES], F32)
-        denominator = keep.tile([P, NODE_TILES], F32)
         inv_sum = keep.tile([P, NODE_TILES], F32)
 
         nadj_codes = keep.tile([P, NODE_TILES, NODE_PASSES, P], U32, align_bytes=64)
         nadj_scales = keep.tile([P, NODE_TILES, NODE_PASSES, P], U8, align_bytes=64)
         query_codes = keep.tile([P, SLICES, NODE_PASSES, FEATURES], U32, align_bytes=64)
         query_scales = keep.tile([P, SLICES, NODE_PASSES, FEATURES], U8, align_bytes=64)
+        wt_grouped = keep.tile([P, FEATURE_TILES, P, PACK], BF16, align_bytes=64)
         wt_codes = keep.tile([P, FEATURES], U32, align_bytes=64)
         wt_scales = keep.tile([P, FEATURES], U8, align_bytes=64)
 
@@ -64,172 +103,279 @@ def tile_gatedspatialattentionlayer_pc_t_kernel(tc, adj, query, Wt, bt, out):
             nc.sync.dma_start(out=adj_sb[:, i, :], in_=adj[i * P : (i + 1) * P, :])
 
         def load_query(s, g):
-            rows = query_slices[s].rearrange("(j p) d -> p j d", p=P)
-            j_range = slice(g * PACK, (g + 1) * PACK)
-            nc.sync.dma_start(out=query_sb[:, s, j_range, :], in_=rows[:, j_range, :])
+            rows = query_slices[s].rearrange("(g p j) d -> g p j d", p=P, j=PACK)
+            nc.sync.dma_start(out=query_sb[:, s, g, :, :], in_=rows[g])
 
-        load_adj(0)
+        def regroup_query(copy, s, g, grouped, d0, d1):
+            copy(
+                out=grouped[:, d0:d1, :].rearrange("p (c i) j -> p c j i", i=4),
+                in_=query_sb[:, s, g, :, d0:d1].rearrange("p j (c i) -> p c j i", i=4),
+            )
+
+        def quantise_query(s, g, grouped):
+            nc.vector.quantize_mx(
+                out=query_codes[:, s, g, :].bitcast(FP8X4),
+                scales=query_scales[:, s, g, :],
+                in_=grouped[:].rearrange("p d j -> p (d j)"),
+            )
+
+        def query_tile():
+            grouped = stage.tile([P, FEATURES, PACK], BF16, align_bytes=64, name="query_grouped")
+            return grouped
+
+        looped = {}
+        nadj = {}
+        nadj_grouped = {}
+
+        folded = {}
+        flipped_words = {}
+        gq_ps = {}
+        out_ps = {}
+        out_sb = {}
+
+        def fold_rows(i):
+            folded[i] = psum.tile([P, P], F32, name="folded", tag="wide")
+            for j in range(NODE_TILES):
+                nc.tensor.matmul(
+                    out=folded[i][:],
+                    lhsT=ident_bf[:],
+                    rhs=adj_sb[:, i, j * P : (j + 1) * P],
+                    start=(j == 0),
+                    stop=False,
+                )
+            nc.tensor.matmul(
+                out=folded[i][:], lhsT=ident_bf[:], rhs=ident_bf[:], start=False, stop=True
+            )
+            looped[i] = stage.tile([P, P], F32, name="looped")
+            nc.gpsimd.tensor_tensor(
+                out=looped[i][:], in0=adj_sb[:, i, i * P : (i + 1) * P], in1=ident_bf[:], op=ALU.add
+            )
+
+        def sum_rows(i):
+            unread = stage.tile([P, P], BF16, name="unread")
+            nc.scalar.activation(
+                out=unread[:], in_=folded[i][:], func=ACT.Copy, accum_out=row_sum[:, i : i + 1]
+            )
+
+        def invert(i):
+            nc.vector.reciprocal(out=inv_sum[:, i : i + 1], in_=row_sum[:, i : i + 1])
+
+        def normalise(i):
+            nadj[i] = stage.tile([P, NODES], BF16, align_bytes=64, name="nadj")
+            nc.vector.tensor_scalar_mul(
+                out=nadj[i][:], in0=adj_sb[:, i, :], scalar1=inv_sum[:, i : i + 1]
+            )
+
+        def mend_diagonal(i):
+            nc.scalar.activation(
+                out=nadj[i][:, i * P : (i + 1) * P],
+                in_=looped[i][:],
+                func=ACT.Copy,
+                scale=inv_sum[:, i : i + 1],
+            )
+
+        def flip_nadj(i):
+            words = nadj[i][:].bitcast(F32)
+            flipped = psum.tile([P, NODE_PASSES * 2, P], F32, name="flipped_words", tag="quad")
+            flipped_words[i] = flipped
+            for g in range(NODE_PASSES):
+                for u in range(2):
+                    nc.tensor.transpose(
+                        flipped[:, 2 * g + u, :],
+                        words[:, g * 2 * P + u : (g + 1) * 2 * P : 2],
+                        ident_f32[:],
+                    )
+
+        def copy_words(i):
+            nadj_grouped[i] = stage.tile([P, NODE_PASSES, P, 2], F32, align_bytes=64, name="nadj_grouped")
+            copy = nc.vector.tensor_copy if i % 2 == 0 else nc.scalar.copy
+            copy(out=nadj_grouped[i][:], in_=flipped_words[i][:].rearrange("p (g u) r -> p g r u", u=2))
+
+        def quantise_nadj(i):
+            nc.vector.quantize_mx(
+                out=nadj_codes[:, i, :, :].rearrange("p g r -> p (g r)").bitcast(FP8X4),
+                scales=nadj_scales[:, i, :, :].rearrange("p g r -> p (g r)"),
+                in_=nadj_grouped[i][:].rearrange("p g r u -> p (g r u)").bitcast(BF16),
+            )
+
+        flipped_wt = {}
+
+        def flip_wt(a):
+            flipped_wt[a] = psum.tile([P, PACK, P], BF16, name="flipped_wt", tag="wide")
+            for t in range(PACK):
+                nc.tensor.transpose(
+                    flipped_wt[a][:, t, :], wt_sb[:, a, t * P : (t + 1) * P], ident_bf[:]
+                )
+
+        def copy_wt(a):
+            nc.scalar.copy(
+                out=wt_grouped[:, a, :, :], in_=flipped_wt[a][:].rearrange("p t r -> p r t")
+            )
+
+        def quantise_wt():
+            nc.vector.quantize_mx(
+                out=wt_codes[:].bitcast(FP8X4),
+                scales=wt_scales[:],
+                in_=wt_grouped[:].rearrange("p a r t -> p (a r t)"),
+            )
+
+        def aggregate(j):
+            s, i = divmod(j, NODE_TILES)
+            gq_ps[j] = psum.tile([P, FEATURE_TILES, P], F32, name="gq_ps", tag="quad")
+            for t in range(FEATURE_TILES):
+                for g in range(NODE_PASSES):
+                    nc.tensor.matmul_mx(
+                        out=gq_ps[j][:, t, :],
+                        lhsT=query_codes[:, s, g, t * P : (t + 1) * P].bitcast(FP8X4),
+                        lhsT_scale=query_scales[:, s, g, t * P : (t + 1) * P],
+                        rhs=nadj_codes[:, i, g, :].bitcast(FP8X4),
+                        rhs_scale=nadj_scales[:, i, g, :],
+                        start=(g == 0),
+                        stop=(g == NODE_PASSES - 1),
+                    )
+
+        def evacuate(j, grouped):
+            nc.scalar.copy(out=grouped, in_=gq_ps[j][:].rearrange("p t r -> p r t"))
+
+        def project(j, codes, scales):
+            out_ps[j] = psum.tile([P, FEATURES], F32, name="out_ps", tag="wide")
+            nc.tensor.matmul_mx(
+                out=out_ps[j][:],
+                lhsT=codes.bitcast(FP8X4),
+                lhsT_scale=scales,
+                rhs=wt_codes[:].bitcast(FP8X4),
+                rhs_scale=wt_scales[:],
+                start=True,
+                stop=True,
+            )
+
+        def add_bias(j):
+            out_sb[j] = results.tile([P, FEATURES], F32, name="result")
+            result = out_sb[j]
+            nc.vector.tensor_tensor(out=result[:], in0=out_ps[j][:], in1=bias_sb[:], op=ALU.add)
+
+        def finish(j):
+            s, i = divmod(j, NODE_TILES)
+            result = out_sb[j]
+            if j % 2 == 0:
+                nc.gpsimd.tensor_scalar(
+                    out=result[:],
+                    in0=result[:],
+                    scalar1=float("inf"),
+                    scalar2=0.0,
+                    op0=ALU.min,
+                    op1=ALU.max,
+                )
+            else:
+                nc.scalar.activation(out=result[:], in_=result[:], func=ACT.Relu)
+            nc.sync.dma_start(out=out_slices[s, i * P : (i + 1) * P, :], in_=result[:])
+
+        ctx.enter_context(tc.manual_schedule())
         load_query(0, 0)
+        load_adj(0)
         load_adj(1)
         load_query(0, 1)
         for i in range(2, NODE_TILES):
             load_adj(i)
         nc.sync.dma_start(out=wt_sb[:], in_=Wt.rearrange("(a p) d -> p a d", p=P))
+        load_query(1, 0)
+        load_query(1, 1)
         nc.sync.dma_start(out=bias_sb[:], in_=bt.partition_broadcast(P))
-        for s in range(1, SLICES):
+        for s in range(2, SLICES):
             for g in range(NODE_PASSES):
                 load_query(s, g)
 
-        def quantise_query(s):
-            for g in range(NODE_PASSES):
-                grouped = stage.tile([P, FEATURES, PACK], BF16, align_bytes=64, name="query_grouped")
-                copy = nc.vector.tensor_copy if s == 0 or g % 2 == 0 else nc.scalar.copy
-                copy(
-                    out=grouped[:].rearrange("p (c i) t -> p c t i", i=4),
-                    in_=query_sb[:, s, g * PACK : (g + 1) * PACK, :].rearrange(
-                        "p t (c i) -> p c t i", i=4
-                    ),
-                )
-                nc.vector.quantize_mx(
-                    out=query_codes[:, s, g, :].bitcast(FP8X4),
-                    scales=query_scales[:, s, g, :],
-                    in_=grouped[:].rearrange("p d t -> p (d t)"),
-                )
+        query_grouped = {}
 
-        def transpose_512(block, diagonal_t):
-            flipped = psum.tile([P, PACK, P], F32, name="flipped", tag="quad")
-            for t in range(PACK):
-                nc.tensor.matmul(
-                    out=flipped[:, t, :],
-                    lhsT=block[:, t * P : (t + 1) * P],
-                    rhs=ident_bf[:],
-                    start=True,
-                    stop=(t != diagonal_t),
-                )
-                if t == diagonal_t:
-                    nc.tensor.matmul(
-                        out=flipped[:, t, :], lhsT=ident_bf[:], rhs=ident_bf[:], start=False, stop=True
-                    )
-            return flipped
+        def query_work(s, what):
+            if what == "regroup0":
+                query_grouped[s, 0] = query_tile()
+                regroup_query(nc.vector.tensor_copy, s, 0, query_grouped[s, 0], 0, FEATURES)
+            elif what == "regroup1v":
+                query_grouped[s, 1] = query_tile()
+                regroup_query(nc.vector.tensor_copy, s, 1, query_grouped[s, 1], 0, FEATURES)
+            elif what == "regroup1a":
+                query_grouped[s, 1] = query_tile()
+                regroup_query(nc.scalar.copy, s, 1, query_grouped[s, 1], 0, FEATURES // 2)
+            elif what == "regroup1b":
+                regroup_query(nc.scalar.copy, s, 1, query_grouped[s, 1], FEATURES // 2, FEATURES)
+            elif what == "quantise0":
+                quantise_query(s, 0, query_grouped[s, 0])
+            elif what == "quantise1":
+                quantise_query(s, 1, query_grouped[s, 1])
+            elif what == "flip_wt":
+                flip_wt(s)
+            elif what == "copy_wt":
+                copy_wt(s)
+            elif what == "quantise_wt":
+                quantise_wt()
 
-        def quantise_nadj(i):
-            unread = stage.tile([P, NODES], BF16, name="unread")
-            nc.scalar.activation(
-                out=unread[:], in_=adj_sb[:, i, :], func=ACT.Copy, accum_out=row_sum[:, i : i + 1]
-            )
-            nc.vector.tensor_scalar_add(
-                out=denominator[:, i : i + 1], in0=row_sum[:, i : i + 1], scalar1=1.0
-            )
-            nc.vector.reciprocal(out=inv_sum[:, i : i + 1], in_=denominator[:, i : i + 1])
-            spread_ps = psum.tile([P, P], F32, name="spread_ps", tag="wide")
-            nc.tensor.matmul(
-                out=spread_ps[:],
-                lhsT=inv_sum[:, i : i + 1].to_broadcast([P, P]),
-                rhs=ident_f32[:],
-                start=True,
-                stop=True,
-            )
-            spread = stage.tile([P, P], F32, name="spread")
-            nc.scalar.copy(out=spread[:], in_=spread_ps[:])
+        group_of = [k for k in range(len(GROUP_SIZES)) for c in range(GROUP_SIZES[k])]
+        group_start = [sum(GROUP_SIZES[:k]) for k in range(len(GROUP_SIZES))]
+        groups = {}
 
-            grouped = stage.tile([P, NODE_PASSES, P, PACK], BF16, align_bytes=64, name="nadj_grouped")
-            for g in range(NODE_PASSES):
-                diagonal_t = i - g * PACK if g == i // PACK else None
-                flipped = transpose_512(adj_sb[:, i, g * K_PASS : (g + 1) * K_PASS], diagonal_t)
-                nc.vector.tensor_tensor(
-                    out=grouped[:, g, :, :],
-                    in0=flipped[:].rearrange("p t r -> p r t"),
-                    in1=spread[:].unsqueeze(2).to_broadcast([P, P, PACK]),
-                    op=ALU.mult,
-                )
+        def gather(j):
+            k = group_of[j]
+            size = GROUP_SIZES[k]
+            c = j - group_start[k]
+            if c == 0:
+                groups[k] = stage.tile([P, 4, P, PACK], BF16, align_bytes=64, name="gq_grouped")
+            evacuate(j, groups[k][:, c, :, :])
+
+        operands = {}
+
+        def quantise_gq(k):
+            size = GROUP_SIZES[k]
+            gq_codes = stage.tile([P, 4 * P], U32, align_bytes=64, name="gq_codes")
+            gq_scales = stage.tile([P, 4 * P], U8, align_bytes=64, name="gq_scales")
             nc.vector.quantize_mx(
-                out=nadj_codes[:, i, :, :].rearrange("p g r -> p (g r)").bitcast(FP8X4),
-                scales=nadj_scales[:, i, :, :].rearrange("p g r -> p (g r)"),
-                in_=grouped[:].rearrange("p g r t -> p (g r t)"),
+                out=gq_codes[:, : size * P].bitcast(FP8X4),
+                scales=gq_scales[:, : size * P],
+                in_=groups[k][:, :size, :, :].rearrange("p c r t -> p (c r t)"),
             )
-
-        def quantise_wt():
-            grouped = keep.tile([P, FEATURE_TILES, P, PACK], BF16, align_bytes=64, name="wt_grouped")
-            for a in range(FEATURE_TILES):
-                flipped = transpose_512(wt_sb[:, a, :], None)
-                nc.scalar.copy(out=grouped[:, a, :, :], in_=flipped[:].rearrange("p t r -> p r t"))
-            nc.vector.quantize_mx(
-                out=wt_codes[:].bitcast(FP8X4),
-                scales=wt_scales[:],
-                in_=grouped[:].rearrange("p a r t -> p (a r t)"),
-            )
-
-        def aggregate(s, h):
-            grouped = stage.tile([P, GROUP, P, PACK], BF16, align_bytes=64, name="gq_grouped")
-            for c in range(GROUP):
-                i = h * GROUP + c
-                gq_ps = psum.tile([P, FEATURE_TILES, P], F32, name="gq_ps", tag="quad")
-                for t in range(FEATURE_TILES):
-                    for g in range(NODE_PASSES):
-                        nc.tensor.matmul_mx(
-                            out=gq_ps[:, t, :],
-                            lhsT=query_codes[:, s, g, t * P : (t + 1) * P].bitcast(FP8X4),
-                            lhsT_scale=query_scales[:, s, g, t * P : (t + 1) * P],
-                            rhs=nadj_codes[:, i, g, :].bitcast(FP8X4),
-                            rhs_scale=nadj_scales[:, i, g, :],
-                            start=(g == 0),
-                            stop=(g == NODE_PASSES - 1),
-                        )
-                nc.scalar.copy(out=grouped[:, c, :, :], in_=gq_ps[:].rearrange("p t r -> p r t"))
-            gq_codes = stage.tile([P, GROUP * P], U32, align_bytes=64, name="gq_codes")
-            gq_scales = stage.tile([P, GROUP * P], U8, align_bytes=64, name="gq_scales")
-            nc.vector.quantize_mx(
-                out=gq_codes[:].bitcast(FP8X4),
-                scales=gq_scales[:],
-                in_=grouped[:].rearrange("p c r t -> p (c r t)"),
-            )
-            return gq_codes, gq_scales
-
-        def project(s, h, gq_codes, gq_scales):
-            for c in range(GROUP):
-                i = h * GROUP + c
-                out_ps = psum.tile([P, FEATURES], F32, name="out_ps", tag="wide")
-                nc.tensor.matmul_mx(
-                    out=out_ps[:],
-                    lhsT=gq_codes[:, c * P : (c + 1) * P].bitcast(FP8X4),
-                    lhsT_scale=gq_scales[:, c * P : (c + 1) * P],
-                    rhs=wt_codes[:].bitcast(FP8X4),
-                    rhs_scale=wt_scales[:],
-                    start=True,
-                    stop=True,
+            for c in range(size):
+                operands[group_start[k] + c] = (
+                    gq_codes[:, c * P : (c + 1) * P],
+                    gq_scales[:, c * P : (c + 1) * P],
                 )
-                rows = out_slices[s, i * P : (i + 1) * P, :]
-                if c < GPSIMD_TILES:
-                    result = own.tile([P, FEATURES], F32, name="own_result")
-                    nc.vector.tensor_tensor(out=result[:], in0=out_ps[:], in1=bias_sb[:], op=ALU.add)
-                    nc.gpsimd.tensor_scalar(
-                        out=result[:],
-                        in0=result[:],
-                        scalar1=float("inf"),
-                        scalar2=0.0,
-                        op0=ALU.min,
-                        op1=ALU.max,
-                    )
-                    nc.gpsimd.dma_start(out=rows, in_=result[:])
-                else:
-                    biased = results.tile([P, FEATURES], F32, name="biased")
-                    nc.vector.tensor_tensor(out=biased[:], in0=out_ps[:], in1=bias_sb[:], op=ALU.add)
-                    result = results.tile([P, FEATURES], F32, name="result")
-                    nc.scalar.activation(out=result[:], in_=biased[:], func=ACT.Relu)
-                    nc.sync.dma_start(out=rows, in_=result[:])
 
-        quantise_query(0)
-        for i in range(NODE_TILES):
-            quantise_nadj(i)
-        quantise_wt()
-
-        pending = None
-        for s in range(SLICES):
-            for h in range(GROUPS):
-                codes_and_scales = aggregate(s, h)
-                if h == 0 and s + 1 < SLICES:
-                    quantise_query(s + 1)
-                if pending is not None:
-                    project(*pending)
-                pending = (s, h) + codes_and_scales
-        project(*pending)
+        stages = (
+            ("invert", invert, NODE_TILES),
+            ("evacuate", gather, SLICES * NODE_TILES),
+            ("aggregate", aggregate, SLICES * NODE_TILES),
+            ("qnadj", quantise_nadj, NODE_TILES),
+            ("words", copy_words, NODE_TILES),
+            ("flip", flip_nadj, NODE_TILES),
+            ("diag", mend_diagonal, NODE_TILES),
+            ("norm", normalise, NODE_TILES),
+            ("sum", sum_rows, NODE_TILES),
+            ("fold", fold_rows, NODE_TILES),
+        )
+        quantised = []
+        projected = []
+        biased = []
+        t = 0
+        stored = 0
+        while stored < SLICES * NODE_TILES:
+            for step, s, what in EXTRA_WORK:
+                if step == t:
+                    query_work(s, what)
+            for j in biased:
+                finish(j)
+                stored += 1
+            for j in projected:
+                add_bias(j)
+            biased = projected
+            width = 1 if t < SLICES * NODE_TILES + LAG["aggregate"] else 2
+            projected = [j for j, step in quantised if step < t][:width]
+            quantised = quantised[len(projected) :]
+            for j in projected:
+                project(j, *operands[j])
+            for k in range(len(GROUP_SIZES)):
+                if group_start[k] + GROUP_SIZES[k] - 1 == t - LAG["evacuate"] - 1:
+                    quantise_gq(k)
+                    quantised = quantised + [(group_start[k] + c, t) for c in range(GROUP_SIZES[k])]
+            for name, stage_of, count in stages:
+                if 0 <= t - LAG[name] < count:
+                    stage_of(t - LAG[name])
+            t += 1

@@ -103,8 +103,10 @@ def tile_gatedspatialattentionlayer_pc_t_kernel(tc, adj, query, Wt, bt, out):
             nc.sync.dma_start(out=adj_sb[:, i, :], in_=adj[i * P : (i + 1) * P, :])
 
         def load_query(s, g):
-            rows = query_slices[s].rearrange("(g p j) d -> g p j d", p=P, j=PACK)
-            nc.sync.dma_start(out=query_sb[:, s, g, :, :], in_=rows[g])
+            rows = query_slices[s].rearrange("(g u p e) d -> g p u (e d)", u=2, p=P, e=2)
+            nc.sync.dma_start(
+                out=query_sb[:, s, g, :, :].rearrange("p (u e) d -> p u (e d)", u=2), in_=rows[g]
+            )
 
         def regroup_query(copy, s, g, grouped, d0, d1):
             copy(
@@ -134,27 +136,32 @@ def tile_gatedspatialattentionlayer_pc_t_kernel(tc, adj, query, Wt, bt, out):
         out_sb = {}
 
         def fold_rows(i):
-            folded[i] = psum.tile([P, P], F32, name="folded", tag="wide")
+            folded[i] = psum.tile([P, 2, P], F32, name="folded", tag="wide")
             for j in range(NODE_TILES):
                 nc.tensor.matmul(
-                    out=folded[i][:],
+                    out=folded[i][:, 0, :],
                     lhsT=ident_bf[:],
                     rhs=adj_sb[:, i, j * P : (j + 1) * P],
                     start=(j == 0),
                     stop=False,
                 )
             nc.tensor.matmul(
-                out=folded[i][:], lhsT=ident_bf[:], rhs=ident_bf[:], start=False, stop=True
+                out=folded[i][:, 0, :], lhsT=ident_bf[:], rhs=ident_bf[:], start=False, stop=True
             )
-            looped[i] = stage.tile([P, P], F32, name="looped")
-            nc.gpsimd.tensor_tensor(
-                out=looped[i][:], in0=adj_sb[:, i, i * P : (i + 1) * P], in1=ident_bf[:], op=ALU.add
+            looped[i] = folded[i][:, 1, :]
+            nc.tensor.matmul(
+                out=looped[i],
+                lhsT=ident_bf[:],
+                rhs=adj_sb[:, i, i * P : (i + 1) * P],
+                start=True,
+                stop=False,
             )
+            nc.tensor.matmul(out=looped[i], lhsT=ident_bf[:], rhs=ident_bf[:], start=False, stop=True)
 
         def sum_rows(i):
             unread = stage.tile([P, P], BF16, name="unread")
             nc.scalar.activation(
-                out=unread[:], in_=folded[i][:], func=ACT.Copy, accum_out=row_sum[:, i : i + 1]
+                out=unread[:], in_=folded[i][:, 0, :], func=ACT.Copy, accum_out=row_sum[:, i : i + 1]
             )
 
         def invert(i):
@@ -169,7 +176,7 @@ def tile_gatedspatialattentionlayer_pc_t_kernel(tc, adj, query, Wt, bt, out):
         def mend_diagonal(i):
             nc.scalar.activation(
                 out=nadj[i][:, i * P : (i + 1) * P],
-                in_=looped[i][:],
+                in_=looped[i],
                 func=ACT.Copy,
                 scale=inv_sum[:, i : i + 1],
             )
@@ -182,7 +189,7 @@ def tile_gatedspatialattentionlayer_pc_t_kernel(tc, adj, query, Wt, bt, out):
                 for u in range(2):
                     nc.tensor.transpose(
                         flipped[:, 2 * g + u, :],
-                        words[:, g * 2 * P + u : (g + 1) * 2 * P : 2],
+                        words[:, (2 * g + u) * P : (2 * g + u + 1) * P],
                         ident_f32[:],
                     )
 
@@ -270,7 +277,6 @@ def tile_gatedspatialattentionlayer_pc_t_kernel(tc, adj, query, Wt, bt, out):
                 nc.scalar.activation(out=result[:], in_=result[:], func=ACT.Relu)
             nc.sync.dma_start(out=out_slices[s, i * P : (i + 1) * P, :], in_=result[:])
 
-        ctx.enter_context(tc.manual_schedule())
         load_query(0, 0)
         load_adj(0)
         load_adj(1)
@@ -297,6 +303,16 @@ def tile_gatedspatialattentionlayer_pc_t_kernel(tc, adj, query, Wt, bt, out):
             elif what == "regroup1a":
                 query_grouped[s, 1] = query_tile()
                 regroup_query(nc.scalar.copy, s, 1, query_grouped[s, 1], 0, FEATURES // 2)
+            elif what == "regroup1av":
+                query_grouped[s, 1] = query_tile()
+                regroup_query(nc.vector.tensor_copy, s, 1, query_grouped[s, 1], 0, FEATURES // 2)
+            elif what == "regroup1bv":
+                regroup_query(nc.vector.tensor_copy, s, 1, query_grouped[s, 1], FEATURES // 2, FEATURES)
+            elif what == "regroup0a":
+                query_grouped[s, 0] = query_tile()
+                regroup_query(nc.scalar.copy, s, 0, query_grouped[s, 0], 0, FEATURES // 2)
+            elif what == "regroup0b":
+                regroup_query(nc.scalar.copy, s, 0, query_grouped[s, 0], FEATURES // 2, FEATURES)
             elif what == "regroup1b":
                 regroup_query(nc.scalar.copy, s, 1, query_grouped[s, 1], FEATURES // 2, FEATURES)
             elif what == "quantise0":
@@ -351,31 +367,52 @@ def tile_gatedspatialattentionlayer_pc_t_kernel(tc, adj, query, Wt, bt, out):
             ("sum", sum_rows, NODE_TILES),
             ("fold", fold_rows, NODE_TILES),
         )
-        quantised = []
-        projected = []
-        biased = []
-        t = 0
-        stored = 0
-        while stored < SLICES * NODE_TILES:
-            for step, s, what in EXTRA_WORK:
-                if step == t:
-                    query_work(s, what)
-            for j in biased:
-                finish(j)
-                stored += 1
-            for j in projected:
-                add_bias(j)
-            biased = projected
+        jobs = {name: (stage_of, count) for name, stage_of, count in stages}
+
+        def run(name, t):
+            stage_of, count = jobs[name]
+            if 0 <= t - LAG[name] < count:
+                stage_of(t - LAG[name])
+
+        state = {"quantised": [], "to_project": [], "to_bias": [], "stored": 0}
+
+        def step(t):
+            to_finish = state["to_bias"]
+            to_bias = state["to_project"]
             width = 1 if t < SLICES * NODE_TILES + LAG["aggregate"] else 2
-            projected = [j for j, step in quantised if step < t][:width]
-            quantised = quantised[len(projected) :]
-            for j in projected:
-                project(j, *operands[j])
+            to_project = [j for j, step in state["quantised"] if step < t][:width]
+            state["quantised"] = state["quantised"][len(to_project) :]
+            state["to_bias"] = to_bias
+            state["to_project"] = to_project
+            run("invert", t)
+            run("evacuate", t)
             for k in range(len(GROUP_SIZES)):
                 if group_start[k] + GROUP_SIZES[k] - 1 == t - LAG["evacuate"] - 1:
                     quantise_gq(k)
-                    quantised = quantised + [(group_start[k] + c, t) for c in range(GROUP_SIZES[k])]
-            for name, stage_of, count in stages:
-                if 0 <= t - LAG[name] < count:
-                    stage_of(t - LAG[name])
+                    state["quantised"] = state["quantised"] + [(group_start[k] + c, t) for c in range(GROUP_SIZES[k])]
+            run("aggregate", t)
+            for j in to_project:
+                project(j, *operands[j])
+            for j in to_bias:
+                add_bias(j)
+            for j in to_finish:
+                finish(j)
+                state["stored"] += 1
+            for when, s, what in EXTRA_WORK:
+                if when == t:
+                    query_work(s, what)
+            run("qnadj", t)
+            run("words", t)
+            run("flip", t)
+            run("diag", t)
+            run("norm", t)
+            run("sum", t)
+            run("fold", t)
+
+        with tc.manual_schedule():
+            for t in range(16):
+                step(t)
+        t = 16
+        while state["stored"] < SLICES * NODE_TILES:
+            step(t)
             t += 1

@@ -136,32 +136,27 @@ def tile_gatedspatialattentionlayer_pc_t_kernel(tc, adj, query, Wt, bt, out):
         out_sb = {}
 
         def fold_rows(i):
-            folded[i] = psum.tile([P, 2, P], F32, name="folded", tag="wide")
+            folded[i] = psum.tile([P, P], F32, name="folded", tag="wide")
             for j in range(NODE_TILES):
                 nc.tensor.matmul(
-                    out=folded[i][:, 0, :],
+                    out=folded[i][:],
                     lhsT=ident_bf[:],
                     rhs=adj_sb[:, i, j * P : (j + 1) * P],
                     start=(j == 0),
                     stop=False,
                 )
             nc.tensor.matmul(
-                out=folded[i][:, 0, :], lhsT=ident_bf[:], rhs=ident_bf[:], start=False, stop=True
+                out=folded[i][:], lhsT=ident_bf[:], rhs=ident_bf[:], start=False, stop=True
             )
-            looped[i] = folded[i][:, 1, :]
-            nc.tensor.matmul(
-                out=looped[i],
-                lhsT=ident_bf[:],
-                rhs=adj_sb[:, i, i * P : (i + 1) * P],
-                start=True,
-                stop=False,
+            looped[i] = stage.tile([P, P], F32, name="looped")
+            nc.vector.tensor_tensor(
+                out=looped[i][:], in0=adj_sb[:, i, i * P : (i + 1) * P], in1=ident_bf[:], op=ALU.add
             )
-            nc.tensor.matmul(out=looped[i], lhsT=ident_bf[:], rhs=ident_bf[:], start=False, stop=True)
 
         def sum_rows(i):
             unread = stage.tile([P, P], BF16, name="unread")
             nc.scalar.activation(
-                out=unread[:], in_=folded[i][:, 0, :], func=ACT.Copy, accum_out=row_sum[:, i : i + 1]
+                out=unread[:], in_=folded[i][:], func=ACT.Copy, accum_out=row_sum[:, i : i + 1]
             )
 
         def invert(i):
@@ -176,7 +171,7 @@ def tile_gatedspatialattentionlayer_pc_t_kernel(tc, adj, query, Wt, bt, out):
         def mend_diagonal(i):
             nc.scalar.activation(
                 out=nadj[i][:, i * P : (i + 1) * P],
-                in_=looped[i],
+                in_=looped[i][:],
                 func=ACT.Copy,
                 scale=inv_sum[:, i : i + 1],
             )
@@ -195,7 +190,7 @@ def tile_gatedspatialattentionlayer_pc_t_kernel(tc, adj, query, Wt, bt, out):
 
         def copy_words(i):
             nadj_grouped[i] = stage.tile([P, NODE_PASSES, P, 2], F32, align_bytes=64, name="nadj_grouped")
-            copy = nc.vector.tensor_copy if i % 2 == 0 else nc.scalar.copy
+            copy = nc.vector.tensor_copy if i > 3 else nc.scalar.copy
             copy(out=nadj_grouped[i][:], in_=flipped_words[i][:].rearrange("p (g u) r -> p g r u", u=2))
 
         def quantise_nadj(i):
@@ -410,9 +405,9 @@ def tile_gatedspatialattentionlayer_pc_t_kernel(tc, adj, query, Wt, bt, out):
             run("fold", t)
 
         with tc.manual_schedule():
-            for t in range(16):
+            for t in range(12):
                 step(t)
-        t = 16
+        t = 12
         while state["stored"] < SLICES * NODE_TILES:
             step(t)
             t += 1

@@ -21,7 +21,6 @@ SLICES = 4
 NODE_TILES = NODES // P
 NODE_PASSES = NODES // K_PASS
 FEATURE_TILES = FEATURES // P
-GROUP_SIZES = (4, 4, 4, 4, 4, 4, 4, 2, 2)
 LAG = {
     "fold": 0,
     "sum": 1,
@@ -33,6 +32,11 @@ LAG = {
     "qnadj": 6,
     "aggregate": 7,
     "evacuate": 8,
+    "qgq": 9,
+    "project": 11,
+    "bias": 12,
+    "finishG": 12,
+    "finishS": 13,
 }
 EXTRA_WORK = (
     (0, 0, "regroup0"),
@@ -40,29 +44,29 @@ EXTRA_WORK = (
     (3, 0, "regroup1v"),
     (5, 0, "quantise1"),
     (7, 0, "flip_wt"),
-    (8, 1, "flip_wt"),
-    (9, 2, "flip_wt"),
-    (10, 3, "flip_wt"),
+    (7, 1, "flip_wt"),
+    (8, 2, "flip_wt"),
+    (8, 3, "flip_wt"),
     (8, 0, "copy_wt"),
-    (9, 1, "copy_wt"),
-    (10, 2, "copy_wt"),
-    (11, 3, "copy_wt"),
-    (12, 0, "quantise_wt"),
-    (9, 1, "regroup0"),
-    (10, 1, "regroup1a"),
-    (11, 1, "quantise0"),
-    (12, 1, "regroup1b"),
-    (14, 1, "quantise1"),
-    (17, 2, "regroup0"),
-    (18, 2, "regroup1a"),
-    (19, 2, "quantise0"),
-    (20, 2, "regroup1b"),
-    (22, 2, "quantise1"),
-    (25, 3, "regroup0"),
-    (26, 3, "regroup1a"),
-    (27, 3, "quantise0"),
-    (28, 3, "regroup1b"),
-    (30, 3, "quantise1"),
+    (8, 1, "copy_wt"),
+    (9, 2, "copy_wt"),
+    (9, 3, "copy_wt"),
+    (10, 0, "quantise_wt"),
+    (8, 1, "regroup0"),
+    (9, 1, "regroup1a"),
+    (10, 1, "quantise0"),
+    (11, 1, "regroup1b"),
+    (13, 1, "quantise1"),
+    (14, 2, "regroup0"),
+    (15, 2, "regroup1a"),
+    (16, 2, "quantise0"),
+    (17, 2, "regroup1b"),
+    (19, 2, "quantise1"),
+    (20, 3, "regroup0"),
+    (21, 3, "regroup1a"),
+    (22, 3, "quantise0"),
+    (23, 3, "regroup1b"),
+    (25, 3, "quantise1"),
 )
 
 FLOPS = 2 * SLICES * NODES * NODES * FEATURES + 2 * SLICES * NODES * FEATURES * FEATURES
@@ -256,10 +260,13 @@ def tile_gatedspatialattentionlayer_pc_t_kernel(tc, adj, query, Wt, bt, out):
             result = out_sb[j]
             nc.vector.tensor_tensor(out=result[:], in0=out_ps[j][:], in1=bias_sb[:], op=ALU.add)
 
+        def on_gpsimd(j):
+            return j % 2 == 0 and j < 28
+
         def finish(j):
             s, i = divmod(j, NODE_TILES)
             result = out_sb[j]
-            if j % 2 == 0:
+            if on_gpsimd(j):
                 nc.gpsimd.tensor_scalar(
                     out=result[:],
                     in0=result[:],
@@ -272,6 +279,7 @@ def tile_gatedspatialattentionlayer_pc_t_kernel(tc, adj, query, Wt, bt, out):
                 nc.scalar.activation(out=result[:], in_=result[:], func=ACT.Relu)
             nc.sync.dma_start(out=out_slices[s, i * P : (i + 1) * P, :], in_=result[:])
 
+        ctx.enter_context(tc.manual_schedule())
         load_query(0, 0)
         load_adj(0)
         load_adj(1)
@@ -321,40 +329,45 @@ def tile_gatedspatialattentionlayer_pc_t_kernel(tc, adj, query, Wt, bt, out):
             elif what == "quantise_wt":
                 quantise_wt()
 
-        group_of = [k for k in range(len(GROUP_SIZES)) for c in range(GROUP_SIZES[k])]
-        group_start = [sum(GROUP_SIZES[:k]) for k in range(len(GROUP_SIZES))]
-        groups = {}
-
-        def gather(j):
-            k = group_of[j]
-            size = GROUP_SIZES[k]
-            c = j - group_start[k]
-            if c == 0:
-                groups[k] = stage.tile([P, 4, P, PACK], BF16, align_bytes=64, name="gq_grouped")
-            evacuate(j, groups[k][:, c, :, :])
-
+        gq_grouped = {}
         operands = {}
 
-        def quantise_gq(k):
-            size = GROUP_SIZES[k]
-            gq_codes = stage.tile([P, 4 * P], U32, align_bytes=64, name="gq_codes")
-            gq_scales = stage.tile([P, 4 * P], U8, align_bytes=64, name="gq_scales")
+        def gather(j):
+            gq_grouped[j] = stage.tile([P, P, PACK], BF16, align_bytes=64, name="gq_grouped")
+            evacuate(j, gq_grouped[j][:])
+
+        def quantise_gq(j):
+            gq_codes = stage.tile([P, P], U32, align_bytes=64, name="gq_codes")
+            gq_scales = stage.tile([P, P], U8, align_bytes=64, name="gq_scales")
             nc.vector.quantize_mx(
-                out=gq_codes[:, : size * P].bitcast(FP8X4),
-                scales=gq_scales[:, : size * P],
-                in_=groups[k][:, :size, :, :].rearrange("p c r t -> p (c r t)"),
+                out=gq_codes[:].bitcast(FP8X4),
+                scales=gq_scales[:],
+                in_=gq_grouped[j][:].rearrange("p r t -> p (r t)"),
             )
-            for c in range(size):
-                operands[group_start[k] + c] = (
-                    gq_codes[:, c * P : (c + 1) * P],
-                    gq_scales[:, c * P : (c + 1) * P],
-                )
+            operands[j] = (gq_codes[:], gq_scales[:])
+
+        def project_tile(j):
+            project(j, *operands[j])
+
+        def finish_on_gpsimd(j):
+            if on_gpsimd(j):
+                finish(j)
+
+        def finish_on_scalar(j):
+            if not on_gpsimd(j):
+                finish(j)
 
         stages = (
             ("invert", invert, NODE_TILES),
             ("evacuate", gather, SLICES * NODE_TILES),
+            ("bias", add_bias, SLICES * NODE_TILES),
+            ("finishG", finish_on_gpsimd, SLICES * NODE_TILES),
+            ("qgq", quantise_gq, SLICES * NODE_TILES),
             ("aggregate", aggregate, SLICES * NODE_TILES),
+            ("project", project_tile, SLICES * NODE_TILES),
             ("qnadj", quantise_nadj, NODE_TILES),
+            ("extra", None, 0),
+            ("finishS", finish_on_scalar, SLICES * NODE_TILES),
             ("words", copy_words, NODE_TILES),
             ("flip", flip_nadj, NODE_TILES),
             ("diag", mend_diagonal, NODE_TILES),
@@ -362,52 +375,11 @@ def tile_gatedspatialattentionlayer_pc_t_kernel(tc, adj, query, Wt, bt, out):
             ("sum", sum_rows, NODE_TILES),
             ("fold", fold_rows, NODE_TILES),
         )
-        jobs = {name: (stage_of, count) for name, stage_of, count in stages}
-
-        def run(name, t):
-            stage_of, count = jobs[name]
-            if 0 <= t - LAG[name] < count:
-                stage_of(t - LAG[name])
-
-        state = {"quantised": [], "to_project": [], "to_bias": [], "stored": 0}
-
-        def step(t):
-            to_finish = state["to_bias"]
-            to_bias = state["to_project"]
-            width = 1 if t < SLICES * NODE_TILES + LAG["aggregate"] else 2
-            to_project = [j for j, step in state["quantised"] if step < t][:width]
-            state["quantised"] = state["quantised"][len(to_project) :]
-            state["to_bias"] = to_bias
-            state["to_project"] = to_project
-            run("invert", t)
-            run("evacuate", t)
-            for k in range(len(GROUP_SIZES)):
-                if group_start[k] + GROUP_SIZES[k] - 1 == t - LAG["evacuate"] - 1:
-                    quantise_gq(k)
-                    state["quantised"] = state["quantised"] + [(group_start[k] + c, t) for c in range(GROUP_SIZES[k])]
-            run("aggregate", t)
-            for j in to_project:
-                project(j, *operands[j])
-            for j in to_bias:
-                add_bias(j)
-            for j in to_finish:
-                finish(j)
-                state["stored"] += 1
-            for when, s, what in EXTRA_WORK:
-                if when == t:
-                    query_work(s, what)
-            run("qnadj", t)
-            run("words", t)
-            run("flip", t)
-            run("diag", t)
-            run("norm", t)
-            run("sum", t)
-            run("fold", t)
-
-        with tc.manual_schedule():
-            for t in range(12):
-                step(t)
-        t = 12
-        while state["stored"] < SLICES * NODE_TILES:
-            step(t)
-            t += 1
+        for t in range(SLICES * NODE_TILES + LAG["finishS"]):
+            for name, stage_of, count in stages:
+                if name == "extra":
+                    for when, s, what in EXTRA_WORK:
+                        if when == t:
+                            query_work(s, what)
+                elif 0 <= t - LAG[name] < count:
+                    stage_of(t - LAG[name])

@@ -41,7 +41,8 @@ LAG = {
 EXTRA_WORK = (
     (0, 0, "regroup0"),
     (2, 0, "quantise0"),
-    (3, 0, "regroup1v"),
+    (3, 0, "regroup1av"),
+    (3, 0, "regroup1b"),
     (5, 0, "quantise1"),
     (7, 0, "flip_wt"),
     (7, 1, "flip_wt"),
@@ -53,9 +54,9 @@ EXTRA_WORK = (
     (9, 3, "copy_wt"),
     (10, 0, "quantise_wt"),
     (8, 1, "regroup0"),
-    (9, 1, "regroup1a"),
+    (9, 1, "regroup1av"),
     (10, 1, "quantise0"),
-    (11, 1, "regroup1b"),
+    (11, 1, "regroup1bv"),
     (13, 1, "quantise1"),
     (14, 2, "regroup0"),
     (15, 2, "regroup1a"),
@@ -194,8 +195,9 @@ def tile_gatedspatialattentionlayer_pc_t_kernel(tc, adj, query, Wt, bt, out):
 
         def copy_words(i):
             nadj_grouped[i] = stage.tile([P, NODE_PASSES, P, 2], F32, align_bytes=64, name="nadj_grouped")
-            copy = nc.vector.tensor_copy if i > 3 else nc.scalar.copy
-            copy(out=nadj_grouped[i][:], in_=flipped_words[i][:].rearrange("p (g u) r -> p g r u", u=2))
+            nc.scalar.copy(
+                out=nadj_grouped[i][:], in_=flipped_words[i][:].rearrange("p (g u) r -> p g r u", u=2)
+            )
 
         def quantise_nadj(i):
             nc.vector.quantize_mx(
@@ -255,10 +257,21 @@ def tile_gatedspatialattentionlayer_pc_t_kernel(tc, adj, query, Wt, bt, out):
                 stop=True,
             )
 
+        def column_parts(j):
+            parts = 2 if j == SLICES * NODE_TILES - 1 else 1
+            width = FEATURES // parts
+            return [slice(part * width, (part + 1) * width) for part in range(parts)]
+
         def add_bias(j):
             out_sb[j] = results.tile([P, FEATURES], F32, name="result")
             result = out_sb[j]
-            nc.vector.tensor_tensor(out=result[:], in0=out_ps[j][:], in1=bias_sb[:], op=ALU.add)
+            for columns in column_parts(j):
+                nc.vector.tensor_tensor(
+                    out=result[:, columns],
+                    in0=out_ps[j][:, columns],
+                    in1=bias_sb[:, columns],
+                    op=ALU.add,
+                )
 
         def on_gpsimd(j):
             return j % 2 == 0 and j < 28
@@ -275,9 +288,14 @@ def tile_gatedspatialattentionlayer_pc_t_kernel(tc, adj, query, Wt, bt, out):
                     op0=ALU.min,
                     op1=ALU.max,
                 )
-            else:
-                nc.scalar.activation(out=result[:], in_=result[:], func=ACT.Relu)
-            nc.sync.dma_start(out=out_slices[s, i * P : (i + 1) * P, :], in_=result[:])
+            for columns in column_parts(j):
+                if not on_gpsimd(j):
+                    nc.scalar.activation(
+                        out=result[:, columns], in_=result[:, columns], func=ACT.Relu
+                    )
+                nc.sync.dma_start(
+                    out=out_slices[s, i * P : (i + 1) * P, columns], in_=result[:, columns]
+                )
 
         ctx.enter_context(tc.manual_schedule())
         load_query(0, 0)

@@ -38,6 +38,7 @@ LAG = {
     "finishG": 12,
     "finishS": 13,
 }
+GPSIMD_COLUMNS = 320
 EXTRA_WORK = (
     (0, 0, "regroup0"),
     (2, 0, "quantise0"),
@@ -148,11 +149,8 @@ def tile_gatedspatialattentionlayer_pc_t_kernel(tc, adj, query, Wt, bt, out):
                     lhsT=ident_bf[:],
                     rhs=adj_sb[:, i, j * P : (j + 1) * P],
                     start=(j == 0),
-                    stop=False,
+                    stop=(j == NODE_TILES - 1),
                 )
-            nc.tensor.matmul(
-                out=folded[i][:], lhsT=ident_bf[:], rhs=ident_bf[:], start=False, stop=True
-            )
             looped[i] = stage.tile([P, P], F32, name="looped")
             nc.vector.tensor_tensor(
                 out=looped[i][:], in0=adj_sb[:, i, i * P : (i + 1) * P], in1=ident_bf[:], op=ALU.add
@@ -161,7 +159,11 @@ def tile_gatedspatialattentionlayer_pc_t_kernel(tc, adj, query, Wt, bt, out):
         def sum_rows(i):
             unread = stage.tile([P, P], BF16, name="unread")
             nc.scalar.activation(
-                out=unread[:], in_=folded[i][:], func=ACT.Copy, accum_out=row_sum[:, i : i + 1]
+                out=unread[:],
+                in_=folded[i][:],
+                func=ACT.Copy,
+                bias=1.0 / P,
+                accum_out=row_sum[:, i : i + 1],
             )
 
         def invert(i):
@@ -273,29 +275,31 @@ def tile_gatedspatialattentionlayer_pc_t_kernel(tc, adj, query, Wt, bt, out):
                     op=ALU.add,
                 )
 
-        def on_gpsimd(j):
-            return j % 2 == 0 and j < 28
-
-        def finish(j):
-            s, i = divmod(j, NODE_TILES)
-            result = out_sb[j]
-            if on_gpsimd(j):
+        def relu_on_gpsimd(j):
+            if j < 30:
                 nc.gpsimd.tensor_scalar(
-                    out=result[:],
-                    in0=result[:],
+                    out=out_sb[j][:, :GPSIMD_COLUMNS],
+                    in0=out_sb[j][:, :GPSIMD_COLUMNS],
                     scalar1=float("inf"),
                     scalar2=0.0,
                     op0=ALU.min,
                     op1=ALU.max,
                 )
-            for columns in column_parts(j):
-                if not on_gpsimd(j):
+
+        def relu_and_store(j):
+            s, i = divmod(j, NODE_TILES)
+            result = out_sb[j]
+            rows = out_slices[s, i * P : (i + 1) * P, :]
+            if j < 30:
+                columns = slice(GPSIMD_COLUMNS, FEATURES)
+                nc.scalar.activation(out=result[:, columns], in_=result[:, columns], func=ACT.Relu)
+                nc.sync.dma_start(out=rows, in_=result[:])
+            else:
+                for columns in column_parts(j):
                     nc.scalar.activation(
                         out=result[:, columns], in_=result[:, columns], func=ACT.Relu
                     )
-                nc.sync.dma_start(
-                    out=out_slices[s, i * P : (i + 1) * P, columns], in_=result[:, columns]
-                )
+                    nc.sync.dma_start(out=rows[:, columns], in_=result[:, columns])
 
         ctx.enter_context(tc.manual_schedule())
         load_query(0, 0)
@@ -329,6 +333,11 @@ def tile_gatedspatialattentionlayer_pc_t_kernel(tc, adj, query, Wt, bt, out):
                 regroup_query(nc.vector.tensor_copy, s, 1, query_grouped[s, 1], 0, FEATURES // 2)
             elif what == "regroup1bv":
                 regroup_query(nc.vector.tensor_copy, s, 1, query_grouped[s, 1], FEATURES // 2, FEATURES)
+            elif what == "regroup0av":
+                query_grouped[s, 0] = query_tile()
+                regroup_query(nc.vector.tensor_copy, s, 0, query_grouped[s, 0], 0, FEATURES // 2)
+            elif what == "regroup0bv":
+                regroup_query(nc.vector.tensor_copy, s, 0, query_grouped[s, 0], FEATURES // 2, FEATURES)
             elif what == "regroup0a":
                 query_grouped[s, 0] = query_tile()
                 regroup_query(nc.scalar.copy, s, 0, query_grouped[s, 0], 0, FEATURES // 2)
@@ -367,25 +376,17 @@ def tile_gatedspatialattentionlayer_pc_t_kernel(tc, adj, query, Wt, bt, out):
         def project_tile(j):
             project(j, *operands[j])
 
-        def finish_on_gpsimd(j):
-            if on_gpsimd(j):
-                finish(j)
-
-        def finish_on_scalar(j):
-            if not on_gpsimd(j):
-                finish(j)
-
         stages = (
             ("invert", invert, NODE_TILES),
             ("evacuate", gather, SLICES * NODE_TILES),
             ("bias", add_bias, SLICES * NODE_TILES),
-            ("finishG", finish_on_gpsimd, SLICES * NODE_TILES),
+            ("finishG", relu_on_gpsimd, SLICES * NODE_TILES),
             ("qgq", quantise_gq, SLICES * NODE_TILES),
             ("aggregate", aggregate, SLICES * NODE_TILES),
             ("project", project_tile, SLICES * NODE_TILES),
             ("qnadj", quantise_nadj, NODE_TILES),
             ("extra", None, 0),
-            ("finishS", finish_on_scalar, SLICES * NODE_TILES),
+            ("finishS", relu_and_store, SLICES * NODE_TILES),
             ("words", copy_words, NODE_TILES),
             ("flip", flip_nadj, NODE_TILES),
             ("diag", mend_diagonal, NODE_TILES),

@@ -64,11 +64,11 @@ EXTRA_WORK = (
     (16, 2, "quantise0"),
     (17, 2, "regroup1b"),
     (19, 2, "quantise1"),
-    (20, 3, "regroup0"),
-    (21, 3, "regroup1a"),
-    (22, 3, "quantise0"),
-    (23, 3, "regroup1b"),
-    (25, 3, "quantise1"),
+    (22, 3, "regroup0"),
+    (23, 3, "regroup1av"),
+    (24, 3, "quantise0"),
+    (25, 3, "regroup1b"),
+    (27, 3, "quantise1"),
 )
 
 FLOPS = 2 * SLICES * NODES * NODES * FEATURES + 2 * SLICES * NODES * FEATURES * FEATURES
@@ -197,9 +197,8 @@ def tile_gatedspatialattentionlayer_pc_t_kernel(tc, adj, query, Wt, bt, out):
 
         def copy_words(i):
             nadj_grouped[i] = stage.tile([P, NODE_PASSES, P, 2], F32, align_bytes=64, name="nadj_grouped")
-            nc.scalar.copy(
-                out=nadj_grouped[i][:], in_=flipped_words[i][:].rearrange("p (g u) r -> p g r u", u=2)
-            )
+            copy = nc.vector.tensor_copy if i == 3 else nc.scalar.copy
+            copy(out=nadj_grouped[i][:], in_=flipped_words[i][:].rearrange("p (g u) r -> p g r u", u=2))
 
         def quantise_nadj(i):
             nc.vector.quantize_mx(
@@ -276,7 +275,7 @@ def tile_gatedspatialattentionlayer_pc_t_kernel(tc, adj, query, Wt, bt, out):
                 )
 
         def relu_on_gpsimd(j):
-            if j < 30:
+            if j < 31:
                 nc.gpsimd.tensor_scalar(
                     out=out_sb[j][:, :GPSIMD_COLUMNS],
                     in0=out_sb[j][:, :GPSIMD_COLUMNS],
@@ -290,7 +289,7 @@ def tile_gatedspatialattentionlayer_pc_t_kernel(tc, adj, query, Wt, bt, out):
             s, i = divmod(j, NODE_TILES)
             result = out_sb[j]
             rows = out_slices[s, i * P : (i + 1) * P, :]
-            if j < 30:
+            if j < 31:
                 columns = slice(GPSIMD_COLUMNS, FEATURES)
                 nc.scalar.activation(out=result[:, columns], in_=result[:, columns], func=ACT.Relu)
                 nc.sync.dma_start(out=rows, in_=result[:])

@@ -30,13 +30,13 @@ LAG = {
     "flip": 4,
     "words": 5,
     "qnadj": 6,
-    "aggregate": 7,
-    "evacuate": 8,
-    "qgq": 9,
-    "project": 11,
-    "bias": 12,
-    "finishG": 12,
-    "finishS": 13,
+    "aggregate": 9,
+    "evacuate": 10,
+    "qgq": 11,
+    "project": 14,
+    "bias": 15,
+    "finishG": 15,
+    "finishS": 17,
 }
 GPSIMD_COLUMNS = 320
 EXTRA_WORK = (

@@ -41,6 +41,7 @@ LAG = {
 GPSIMD_COLUMNS = 320
 EXTRA_WORK = (
     (0, 0, "regroup0"),
+    (0, 0, "spread_bias"),
     (2, 0, "quantise0"),
     (3, 0, "regroup1av"),
     (3, 0, "regroup1b"),
@@ -94,6 +95,8 @@ def tile_gatedspatialattentionlayer_pc_t_kernel(tc, adj, query, Wt, bt, out):
         query_sb = keep.tile([P, SLICES, NODE_PASSES, PACK, FEATURES], BF16)
         wt_sb = keep.tile([P, FEATURE_TILES, FEATURES], BF16)
         bias_sb = keep.tile([P, FEATURES], BF16)
+        bias_row = keep.tile([P, FEATURES], BF16)
+        ones = keep.tile([P, P], BF16)
         row_sum = keep.tile([P, NODE_TILES], F32)
         inv_sum = keep.tile([P, NODE_TILES], F32)
 
@@ -301,6 +304,9 @@ def tile_gatedspatialattentionlayer_pc_t_kernel(tc, adj, query, Wt, bt, out):
                     nc.sync.dma_start(out=rows[:, columns], in_=result[:, columns])
 
         ctx.enter_context(tc.manual_schedule())
+        nc.vector.memset(bias_row[:], 0.0)
+        nc.vector.memset(ones[:], 1.0)
+        nc.scalar.dma_start(out=bias_row[0:1, :], in_=bt.rearrange("(o d) -> o d", o=1))
         load_query(0, 0)
         load_adj(0)
         load_adj(1)
@@ -310,7 +316,6 @@ def tile_gatedspatialattentionlayer_pc_t_kernel(tc, adj, query, Wt, bt, out):
         nc.sync.dma_start(out=wt_sb[:], in_=Wt.rearrange("(a p) d -> p a d", p=P))
         load_query(1, 0)
         load_query(1, 1)
-        nc.sync.dma_start(out=bias_sb[:], in_=bt.partition_broadcast(P))
         for s in range(2, SLICES):
             for g in range(NODE_PASSES):
                 load_query(s, g)
@@ -352,6 +357,12 @@ def tile_gatedspatialattentionlayer_pc_t_kernel(tc, adj, query, Wt, bt, out):
                 flip_wt(s)
             elif what == "copy_wt":
                 copy_wt(s)
+            elif what == "spread_bias":
+                bias_ps = psum.tile([P, FEATURES], F32, name="bias_ps", tag="wide")
+                nc.tensor.matmul(
+                    out=bias_ps[:], lhsT=ones[:], rhs=bias_row[:], start=True, stop=True
+                )
+                nc.scalar.copy(out=bias_sb[:], in_=bias_ps[:])
             elif what == "quantise_wt":
                 quantise_wt()
 

@@ -40,8 +40,8 @@ LAG = {
 }
 GPSIMD_COLUMNS = 320
 EXTRA_WORK = (
-    (0, 0, "regroup0"),
     (0, 0, "spread_bias"),
+    (0, 0, "regroup0"),
     (2, 0, "quantise0"),
     (3, 0, "regroup1av"),
     (3, 0, "regroup1b"),
@@ -306,8 +306,8 @@ def tile_gatedspatialattentionlayer_pc_t_kernel(tc, adj, query, Wt, bt, out):
         ctx.enter_context(tc.manual_schedule())
         nc.vector.memset(bias_row[:], 0.0)
         nc.vector.memset(ones[:], 1.0)
-        nc.scalar.dma_start(out=bias_row[0:1, :], in_=bt.rearrange("(o d) -> o d", o=1))
         load_query(0, 0)
+        nc.sync.dma_start(out=bias_row[0:1, :], in_=bt.rearrange("(o d) -> o d", o=1))
         load_adj(0)
         load_adj(1)
         load_query(0, 1)

from contextlib import ExitStack

import concourse.mybir as mybir
from concourse.masks import make_identity

F32 = mybir.dt.float32
BF16 = mybir.dt.bfloat16
U32 = mybir.dt.uint32
U8 = mybir.dt.uint8
FP8X4 = mybir.dt.float8_e4m3fn_x4
ACT = mybir.ActivationFunctionType
ALU = mybir.AluOpType

P = 128
PACK = 4
K_PASS = P * PACK

NODES = 1024
FEATURES = 512
SLICES = 4
NODE_TILES = NODES // P
NODE_PASSES = NODES // K_PASS
FEATURE_TILES = FEATURES // P
LAG = {
    "fold": 0,
    "sum": 1,
    "invert": 2,
    "norm": 2,
    "diag": 3,
    "flip": 4,
    "words": 5,
    "qnadj": 6,
    "aggregate": 9,
    "evacuate": 10,
    "qgq": 11,
    "project": 14,
    "bias": 15,
    "finishG": 15,
    "finishS": 17,
}
GPSIMD_COLUMNS = 320
EXTRA_WORK = (
    (0, 0, "spread_bias"),
    (0, 0, "regroup0"),
    (2, 0, "quantise0"),
    (3, 0, "regroup1av"),
    (3, 0, "regroup1b"),
    (5, 0, "quantise1"),
    (7, 0, "flip_wt"),
    (7, 1, "flip_wt"),
    (8, 2, "flip_wt"),
    (8, 3, "flip_wt"),
    (8, 0, "copy_wt"),
    (8, 1, "copy_wt"),
    (9, 2, "copy_wt"),
    (9, 3, "copy_wt"),
    (10, 0, "quantise_wt"),
    (8, 1, "regroup0"),
    (9, 1, "regroup1av"),
    (10, 1, "quantise0"),
    (11, 1, "regroup1bv"),
    (13, 1, "quantise1"),
    (14, 2, "regroup0"),
    (15, 2, "regroup1a"),
    (16, 2, "quantise0"),
    (17, 2, "regroup1b"),
    (19, 2, "quantise1"),
    (22, 3, "regroup0"),
    (23, 3, "regroup1av"),
    (24, 3, "quantise0"),
    (25, 3, "regroup1b"),
    (27, 3, "quantise1"),
)

FLOPS = 2 * SLICES * NODES * NODES * FEATURES + 2 * SLICES * NODES * FEATURES * FEATURES


def tile_gatedspatialattentionlayer_pc_t_kernel(tc, adj, query, Wt, bt, out):
    nc = tc.nc
    query_slices = query.rearrange("b t n d -> (b t) n d")
    out_slices = out.rearrange("b t n o -> (b t) n o")

    with ExitStack() as ctx:
        keep = ctx.enter_context(tc.tile_pool(name="keep", bufs=1))
        stage = ctx.enter_context(tc.tile_pool(name="stage", bufs=4))
        results = ctx.enter_context(tc.tile_pool(name="results", bufs=8))
        psum = ctx.enter_context(tc.psum_pool(name="psum", bufs=4))

        ident_bf = keep.tile([P, P], BF16)
        make_identity(nc, ident_bf[:])
        ident_f32 = keep.tile([P, P], F32)
        make_identity(nc, ident_f32[:])

        adj_sb = keep.tile([P, NODE_TILES, NODES], BF16)
        query_sb = keep.tile([P, SLICES, NODE_PASSES, PACK, FEATURES], BF16)
        wt_sb = keep.tile([P, FEATURE_TILES, FEATURES], BF16)
        bias_sb = keep.tile([P, FEATURES], BF16)
        bias_row = keep.tile([P, FEATURES], BF16)
        ones = keep.tile([P, P], BF16)
        row_sum = keep.tile([P, NODE_TILES], F32)
        inv_sum = keep.tile([P, NODE_TILES], F32)

        nadj_codes = keep.tile([P, NODE_TILES, NODE_PASSES, P], U32, align_bytes=64)
        nadj_scales = keep.tile([P, NODE_TILES, NODE_PASSES, P], U8, align_bytes=64)
        query_codes = keep.tile([P, SLICES, NODE_PASSES, FEATURES], U32, align_bytes=64)
        query_scales = keep.tile([P, SLICES, NODE_PASSES, FEATURES], U8, align_bytes=64)
        wt_grouped = keep.tile([P, FEATURE_TILES, P, PACK], BF16, align_bytes=64)
        wt_codes = keep.tile([P, FEATURES], U32, align_bytes=64)
        wt_scales = keep.tile([P, FEATURES], U8, align_bytes=64)

        def load_adj(i):
            nc.sync.dma_start(out=adj_sb[:, i, :], in_=adj[i * P : (i + 1) * P, :])

        def load_query(s, g):
            rows = query_slices[s].rearrange("(g u p e) d -> g p u (e d)", u=2, p=P, e=2)
            nc.sync.dma_start(
                out=query_sb[:, s, g, :, :].rearrange("p (u e) d -> p u (e d)", u=2), in_=rows[g]
            )

        def regroup_query(copy, s, g, grouped, d0, d1):
            copy(
                out=grouped[:, d0:d1, :].rearrange("p (c i) j -> p c j i", i=4),
                in_=query_sb[:, s, g, :, d0:d1].rearrange("p j (c i) -> p c j i", i=4),
            )

        def quantise_query(s, g, grouped):
            nc.vector.quantize_mx(
                out=query_codes[:, s, g, :].bitcast(FP8X4),
                scales=query_scales[:, s, g, :],
                in_=grouped[:].rearrange("p d j -> p (d j)"),
            )

        def query_tile():
            grouped = stage.tile([P, FEATURES, PACK], BF16, align_bytes=64, name="query_grouped")
            return grouped

        looped = {}
        nadj = {}
        nadj_grouped = {}

        folded = {}
        flipped_words = {}
        gq_ps = {}
        out_ps = {}
        out_sb = {}

        def fold_rows(i):
            folded[i] = psum.tile([P, P], F32, name="folded", tag="wide")
            for j in range(NODE_TILES):
                nc.tensor.matmul(
                    out=folded[i][:],
                    lhsT=ident_bf[:],
                    rhs=adj_sb[:, i, j * P : (j + 1) * P],
                    start=(j == 0),
                    stop=(j == NODE_TILES - 1),
                )
            looped[i] = stage.tile([P, P], F32, name="looped")
            nc.vector.tensor_tensor(
                out=looped[i][:], in0=adj_sb[:, i, i * P : (i + 1) * P], in1=ident_bf[:], op=ALU.add
            )

        def sum_rows(i):
            unread = stage.tile([P, P], BF16, name="unread")
            nc.scalar.activation(
                out=unread[:],
                in_=folded[i][:],
                func=ACT.Copy,
                bias=1.0 / P,
                accum_out=row_sum[:, i : i + 1],
            )

        def invert(i):
            nc.vector.reciprocal(out=inv_sum[:, i : i + 1], in_=row_sum[:, i : i + 1])

        def normalise(i):
            nadj[i] = stage.tile([P, NODES], BF16, align_bytes=64, name="nadj")
            nc.vector.tensor_scalar_mul(
                out=nadj[i][:], in0=adj_sb[:, i, :], scalar1=inv_sum[:, i : i + 1]
            )

        def mend_diagonal(i):
            nc.scalar.activation(
                out=nadj[i][:, i * P : (i + 1) * P],
                in_=looped[i][:],
                func=ACT.Copy,
                scale=inv_sum[:, i : i + 1],
            )

        def flip_nadj(i):
            words = nadj[i][:].bitcast(F32)
            flipped = psum.tile([P, NODE_PASSES * 2, P], F32, name="flipped_words", tag="quad")
            flipped_words[i] = flipped
            for g in range(NODE_PASSES):
                for u in range(2):
                    nc.tensor.transpose(
                        flipped[:, 2 * g + u, :],
                        words[:, (2 * g + u) * P : (2 * g + u + 1) * P],
                        ident_f32[:],
                    )

        def copy_words(i):
            nadj_grouped[i] = stage.tile([P, NODE_PASSES, P, 2], F32, align_bytes=64, name="nadj_grouped")
            copy = nc.vector.tensor_copy if i == 3 else nc.scalar.copy
            copy(out=nadj_grouped[i][:], in_=flipped_words[i][:].rearrange("p (g u) r -> p g r u", u=2))

        def quantise_nadj(i):
            nc.vector.quantize_mx(
                out=nadj_codes[:, i, :, :].rearrange("p g r -> p (g r)").bitcast(FP8X4),
                scales=nadj_scales[:, i, :, :].rearrange("p g r -> p (g r)"),
                in_=nadj_grouped[i][:].rearrange("p g r u -> p (g r u)").bitcast(BF16),
            )

        flipped_wt = {}

        def flip_wt(a):
            flipped_wt[a] = psum.tile([P, PACK, P], BF16, name="flipped_wt", tag="wide")
            for t in range(PACK):
                nc.tensor.transpose(
                    flipped_wt[a][:, t, :], wt_sb[:, a, t * P : (t + 1) * P], ident_bf[:]
                )

        def copy_wt(a):
            nc.scalar.copy(
                out=wt_grouped[:, a, :, :], in_=flipped_wt[a][:].rearrange("p t r -> p r t")
            )

        def quantise_wt():
            nc.vector.quantize_mx(
                out=wt_codes[:].bitcast(FP8X4),
                scales=wt_scales[:],
                in_=wt_grouped[:].rearrange("p a r t -> p (a r t)"),
            )

        def aggregate(j):
            s, i = divmod(j, NODE_TILES)
            gq_ps[j] = psum.tile([P, FEATURE_TILES, P], F32, name="gq_ps", tag="quad")
            for t in range(FEATURE_TILES):
                for g in range(NODE_PASSES):
                    nc.tensor.matmul_mx(
                        out=gq_ps[j][:, t, :],
                        lhsT=query_codes[:, s, g, t * P : (t + 1) * P].bitcast(FP8X4),
                        lhsT_scale=query_scales[:, s, g, t * P : (t + 1) * P],
                        rhs=nadj_codes[:, i, g, :].bitcast(FP8X4),
                        rhs_scale=nadj_scales[:, i, g, :],
                        start=(g == 0),
                        stop=(g == NODE_PASSES - 1),
                    )

        def evacuate(j, grouped):
            nc.scalar.copy(out=grouped, in_=gq_ps[j][:].rearrange("p t r -> p r t"))

        def project(j, codes, scales):
            out_ps[j] = psum.tile([P, FEATURES], F32, name="out_ps", tag="wide")
            nc.tensor.matmul_mx(
                out=out_ps[j][:],
                lhsT=codes.bitcast(FP8X4),
                lhsT_scale=scales,
                rhs=wt_codes[:].bitcast(FP8X4),
                rhs_scale=wt_scales[:],
                start=True,
                stop=True,
            )

        def column_parts(j):
            parts = 2 if j == SLICES * NODE_TILES - 1 else 1
            width = FEATURES // parts
            return [slice(part * width, (part + 1) * width) for part in range(parts)]

        def add_bias(j):
            out_sb[j] = results.tile([P, FEATURES], F32, name="result")
            result = out_sb[j]
            for columns in column_parts(j):
                nc.vector.tensor_tensor(
                    out=result[:, columns],
                    in0=out_ps[j][:, columns],
                    in1=bias_sb[:, columns],
                    op=ALU.add,
                )

        def relu_on_gpsimd(j):
            if j < 31:
                nc.gpsimd.tensor_scalar(
                    out=out_sb[j][:, :GPSIMD_COLUMNS],
                    in0=out_sb[j][:, :GPSIMD_COLUMNS],
                    scalar1=float("inf"),
                    scalar2=0.0,
                    op0=ALU.min,
                    op1=ALU.max,
                )

        def relu_and_store(j):
            s, i = divmod(j, NODE_TILES)
            result = out_sb[j]
            rows = out_slices[s, i * P : (i + 1) * P, :]
            if j < 31:
                columns = slice(GPSIMD_COLUMNS, FEATURES)
                nc.scalar.activation(out=result[:, columns], in_=result[:, columns], func=ACT.Relu)
                nc.sync.dma_start(out=rows, in_=result[:])
            else:
                for columns in column_parts(j):
                    nc.scalar.activation(
                        out=result[:, columns], in_=result[:, columns], func=ACT.Relu
                    )
                    nc.sync.dma_start(out=rows[:, columns], in_=result[:, columns])

        ctx.enter_context(tc.manual_schedule())
        nc.vector.memset(bias_row[:], 0.0)
        nc.vector.memset(ones[:], 1.0)
        load_query(0, 0)
        nc.sync.dma_start(out=bias_row[0:1, :], in_=bt.rearrange("(o d) -> o d", o=1))
        load_adj(0)
        load_adj(1)
        load_query(0, 1)
        for i in range(2, NODE_TILES):
            load_adj(i)
        nc.sync.dma_start(out=wt_sb[:], in_=Wt.rearrange("(a p) d -> p a d", p=P))
        load_query(1, 0)
        load_query(1, 1)
        for s in range(2, SLICES):
            for g in range(NODE_PASSES):
                load_query(s, g)

        query_grouped = {}

        def query_work(s, what):
            if what == "regroup0":
                query_grouped[s, 0] = query_tile()
                regroup_query(nc.vector.tensor_copy, s, 0, query_grouped[s, 0], 0, FEATURES)
            elif what == "regroup1v":
                query_grouped[s, 1] = query_tile()
                regroup_query(nc.vector.tensor_copy, s, 1, query_grouped[s, 1], 0, FEATURES)
            elif what == "regroup1a":
                query_grouped[s, 1] = query_tile()
                regroup_query(nc.scalar.copy, s, 1, query_grouped[s, 1], 0, FEATURES // 2)
            elif what == "regroup1av":
                query_grouped[s, 1] = query_tile()
                regroup_query(nc.vector.tensor_copy, s, 1, query_grouped[s, 1], 0, FEATURES // 2)
            elif what == "regroup1bv":
                regroup_query(nc.vector.tensor_copy, s, 1, query_grouped[s, 1], FEATURES // 2, FEATURES)
            elif what == "regroup0av":
                query_grouped[s, 0] = query_tile()
                regroup_query(nc.vector.tensor_copy, s, 0, query_grouped[s, 0], 0, FEATURES // 2)
            elif what == "regroup0bv":
                regroup_query(nc.vector.tensor_copy, s, 0, query_grouped[s, 0], FEATURES // 2, FEATURES)
            elif what == "regroup0a":
                query_grouped[s, 0] = query_tile()
                regroup_query(nc.scalar.copy, s, 0, query_grouped[s, 0], 0, FEATURES // 2)
            elif what == "regroup0b":
                regroup_query(nc.scalar.copy, s, 0, query_grouped[s, 0], FEATURES // 2, FEATURES)
            elif what == "regroup1b":
                regroup_query(nc.scalar.copy, s, 1, query_grouped[s, 1], FEATURES // 2, FEATURES)
            elif what == "quantise0":
                quantise_query(s, 0, query_grouped[s, 0])
            elif what == "quantise1":
                quantise_query(s, 1, query_grouped[s, 1])
            elif what == "flip_wt":
                flip_wt(s)
            elif what == "copy_wt":
                copy_wt(s)
            elif what == "spread_bias":
                bias_ps = psum.tile([P, FEATURES], F32, name="bias_ps", tag="wide")
                nc.tensor.matmul(
                    out=bias_ps[:], lhsT=ones[:], rhs=bias_row[:], start=True, stop=True
                )
                nc.scalar.copy(out=bias_sb[:], in_=bias_ps[:])
            elif what == "quantise_wt":
                quantise_wt()

        gq_grouped = {}
        operands = {}

        def gather(j):
            gq_grouped[j] = stage.tile([P, P, PACK], BF16, align_bytes=64, name="gq_grouped")
            evacuate(j, gq_grouped[j][:])

        def quantise_gq(j):
            gq_codes = stage.tile([P, P], U32, align_bytes=64, name="gq_codes")
            gq_scales = stage.tile([P, P], U8, align_bytes=64, name="gq_scales")
            nc.vector.quantize_mx(
                out=gq_codes[:].bitcast(FP8X4),
                scales=gq_scales[:],
                in_=gq_grouped[j][:].rearrange("p r t -> p (r t)"),
            )
            operands[j] = (gq_codes[:], gq_scales[:])

        def project_tile(j):
            project(j, *operands[j])

        stages = (
            ("invert", invert, NODE_TILES),
            ("evacuate", gather, SLICES * NODE_TILES),
            ("bias", add_bias, SLICES * NODE_TILES),
            ("finishG", relu_on_gpsimd, SLICES * NODE_TILES),
            ("qgq", quantise_gq, SLICES * NODE_TILES),
            ("aggregate", aggregate, SLICES * NODE_TILES),
            ("project", project_tile, SLICES * NODE_TILES),
            ("qnadj", quantise_nadj, NODE_TILES),
            ("extra", None, 0),
            ("finishS", relu_and_store, SLICES * NODE_TILES),
            ("words", copy_words, NODE_TILES),
            ("flip", flip_nadj, NODE_TILES),
            ("diag", mend_diagonal, NODE_TILES),
            ("norm", normalise, NODE_TILES),
            ("sum", sum_rows, NODE_TILES),
            ("fold", fold_rows, NODE_TILES),
        )
        for t in range(SLICES * NODE_TILES + LAG["finishS"]):
            for name, stage_of, count in stages:
                if name == "extra":
                    for when, s, what in EXTRA_WORK:
                        if when == t:
                            query_work(s, what)
                elif 0 <= t - LAG[name] < count:
                    stage_of(t - LAG[name])
